import numpy as np
import ml_dtypes


def mxq(x, axis, fmt="e4m3"):
    dtype, down = {"e4m3": (ml_dtypes.float8_e4m3fn, 7), "e5m2": (ml_dtypes.float8_e5m2, 14)}[fmt]
    v = np.moveaxis(np.asarray(x, np.float32).astype(ml_dtypes.bfloat16).astype(np.float64), axis, -1)
    blocks = v.reshape(v.shape[:-1] + (-1, 32))
    amax = np.abs(blocks).max(-1, keepdims=True)
    byte = np.maximum(np.where(amax > 0, np.frexp(amax)[1] - 1 + 127, 0) - down, 1)
    scale = np.exp2(byte - 127.0)
    codes = (blocks / scale).astype(np.float32).astype(dtype).astype(np.float64)
    return np.moveaxis((codes * scale).reshape(v.shape), -1, axis)


WIDE = False


def mx_kscale(k):
    if not WIDE:
        return np.ones(k)
    levels = np.array([10, -10, 5, -5, 0])
    a = np.random.permutation(np.resize(levels, k // 512 * 4)).reshape(k // 512, 4)
    idx = np.arange(k)
    return np.exp2(a[idx // 512, idx % 128 // 32])


BF16 = ml_dtypes.bfloat16


def bf(x):
    return np.asarray(x, np.float32).astype(BF16)


def f64(x):
    return np.asarray(x).astype(np.float64)


B, S, HID, H, KV, D, T = 1, 512, 2048, 16, 2, 128, 512
DQ = H * D
DKV = KV * D
OUT = DQ + 2 * DKV
THETA = 1e4


def make_pos_emb():
    i = np.repeat(np.arange(D // 2), 2)
    freq = np.power(THETA, -i * 2.0 / D)
    t = freq[:, None] * f64(np.arange(T))[None, :]
    cos = np.cos(t)
    sin = np.sin(t)
    sin[0::2] *= -1.0
    return np.concatenate([cos, sin], axis=0).T


def flip_pairs(x):
    return x.reshape(x.shape[:-1] + (D // 2, 2))[..., ::-1].reshape(x.shape)


def apply_rope(x, pe):
    return x * pe[:, :D] + flip_pairs(x) * pe[:, D:]


def setup_inputs():
    s = mx_kscale(HID)
    return {"tensor": bf(np.random.standard_normal((B, S, HID)) * s),
            "w_qkv": bf(np.random.standard_normal((OUT, HID)) * 1.5 / np.sqrt(HID) / s[None, :]),
            "b_qkv": bf(np.random.standard_normal(OUT) * 0.3),
            "pos_emb": bf(make_pos_emb())}


def reference(tensor, w_qkv, b_qkv, pos_emb):
    qkv = (mxq(f64(tensor), 2, "e4m3") @ mxq(f64(w_qkv), 1, "e4m3").T) + f64(b_qkv)
    q = qkv[..., :DQ].reshape(B, S, H, D).transpose(0, 2, 1, 3)
    k = qkv[..., DQ:DQ + DKV].reshape(B, S, KV, D).transpose(0, 2, 1, 3)
    v = qkv[..., DQ + DKV:].reshape(B, S, KV, D).transpose(0, 2, 1, 3)
    pe = f64(pos_emb)[:S]
    return apply_rope(q, pe), apply_rope(k, pe), v

@@ -1,0 +1,204 @@
+from contextlib import ExitStack
+
+import concourse.mybir as mybir
+from concourse.masks import make_identity
+
+F32 = mybir.dt.float32
+BF16 = mybir.dt.bfloat16
+U32 = mybir.dt.uint32
+U8 = mybir.dt.uint8
+FP8X4 = mybir.dt.float8_e4m3fn_x4
+IDENT = mybir.ActivationFunctionType.Identity
+MUL = mybir.AluOpType.mult
+ADD = mybir.AluOpType.add
+
+P = 128
+S = 512
+HID = 2048
+D = 128
+NH = 20
+NROPE = 18
+NT = S // P
+NG = HID // 512
+FLOPS = 2 * S * NH * D * HID
+
+HPC = 2
+BL = 1
+GADD = []
+
+
+def tile_multiqueryattention_pa_kernel(tc, tensor, w_qkv, b_qkv, pos_emb, out_0, out_1, out_2):
+    nc = tc.nc
+    with ExitStack() as ctx:
+        const = ctx.enter_context(tc.tile_pool(name="const", bufs=1))
+        raw = ctx.enter_context(tc.tile_pool(name="raw", bufs=1))
+        grp = ctx.enter_context(tc.tile_pool(name="grp", bufs=4))
+        cod = ctx.enter_context(tc.tile_pool(name="cod", bufs=2 * HPC + 1))
+        wrk = ctx.enter_context(tc.tile_pool(name="wrk", bufs=2 * HPC))
+        yout = ctx.enter_context(tc.tile_pool(name="yout", bufs=8))
+        ps_f = ctx.enter_context(tc.psum_pool(name="ps_f", bufs=4))
+        ps_a = ctx.enter_context(tc.psum_pool(name="ps_a", bufs=2))
+        ps_b = ctx.enter_context(tc.psum_pool(name="ps_b", bufs=2))
+        ctx.enter_context(tc.manual_schedule())
+
+        brow = const.tile([P, D], BF16, name="brow")
+        nc.scalar.dma_start(out=brow[0:NH, :], in_=b_qkv.rearrange("(h d) -> h d", d=D))
+        xv = tensor.rearrange("b (p t) k -> (b t) p k", t=NT)
+        units = {}
+        for t in range(NT):
+            xr = raw.tile([P, HID], BF16, name="xraw%d" % t)
+            nc.sync.dma_start(out=xr[:], in_=xv[t])
+            units[("x", t)] = xr
+        pe = const.tile([P, NT, 2 * D], BF16, name="pe")
+        for h in range(NH):
+            wr = raw.tile([P, HID], BF16, name="wraw%d" % h)
+            nc.sync.dma_start(out=wr[:], in_=w_qkv[h * D:(h + 1) * D, :])
+            units[("w", h)] = wr
+            if h == 1:
+                nc.sync.dma_start(out=pe[:], in_=pos_emb.rearrange("(p t) c -> p t c", t=NT))
+
+        ident = const.tile([P, P], F32, name="ident")
+        make_identity(nc, ident[:])
+        brow32 = const.tile([P, P], F32, name="brow32")
+        nc.vector.memset(brow32[:], 0.0)
+        nc.vector.tensor_copy(out=brow32[0:NH, :], in_=brow[0:NH, :])
+        bias_col = const.tile([P, 32], F32, name="bias_col")
+
+        xc = const.tile([P, NG * S], U32, name="xc", align_bytes=64)
+        xs = const.tile([P, NG * S], U8, name="xs", align_bytes=64)
+
+        banks = {}
+        grouped = {}
+        codes = {}
+        acc = {}
+        tts = {}
+        back = {}
+        ys = {}
+        bps = {}
+
+        def fwd_t(u):
+            src = units[u][:].bitcast(F32)
+            pair = []
+            for b in range(2):
+                f = ps_f.tile([P, 512], F32, name="f", tag="f")
+                for q in range(4):
+                    j = 4 * b + q
+                    nc.tensor.transpose(out=f[:, q * P:(q + 1) * P], in_=src[:, j * P:(j + 1) * P], identity=ident[:])
+                pair.append(f)
+            banks[u] = pair
+
+        def f_evac(u, engines):
+            g = grp.tile([P, HID], BF16, name="g", tag="g", align_bytes=64)
+            gw = g[:].bitcast(F32)
+            for b in range(2):
+                dst = gw[:, b * 512:(b + 1) * 512].rearrange("p (g r u) -> p g r u", g=2, u=2)
+                src = banks[u][b][:].rearrange("p (g u r) -> p g r u", g=2, u=2)
+                if engines[b] == "s":
+                    nc.scalar.copy(out=dst, in_=src)
+                else:
+                    nc.vector.tensor_copy(out=dst, in_=src)
+            grouped[u] = g
+
+        def quant(u):
+            g = grouped[u]
+            if u[0] == "x":
+                t = u[1]
+                for k in range(NG):
+                    c0 = k * S + t * P
+                    nc.vector.quantize_mx(out=xc[:, c0:c0 + P].bitcast(FP8X4), scales=xs[:, c0:c0 + P],
+                                          in_=g[:, k * 512:(k + 1) * 512])
+            else:
+                wc = cod.tile([P, NG * P], U32, name="wc", tag="wc", align_bytes=64)
+                ws = cod.tile([P, NG * P], U8, name="ws", tag="ws", align_bytes=64)
+                nc.vector.quantize_mx(out=wc[:].bitcast(FP8X4), scales=ws[:], in_=g[:])
+                codes[u[1]] = (wc, ws)
+
+        def mx(h):
+            wc, ws = codes[h]
+            a = ps_a.tile([P, S], F32, name="a", tag="a")
+            for k in range(NG):
+                nc.tensor.matmul_mx(out=a[:], lhsT=wc[:, k * P:(k + 1) * P].bitcast(FP8X4),
+                                    lhsT_scale=ws[:, k * P:(k + 1) * P],
+                                    rhs=xc[:, k * S:(k + 1) * S].bitcast(FP8X4),
+                                    rhs_scale=xs[:, k * S:(k + 1) * S],
+                                    start=(k == 0), stop=(k == NG - 1))
+            acc[h] = a
+
+        def b_evac(h):
+            tt = wrk.tile([P, S], F32, name="tt", tag="tt")
+            nc.scalar.activation(out=tt[:], in_=acc[h][:], func=IDENT, bias=bias_col[:, h:h + 1], scale=1.0)
+            tts[h] = tt
+
+        def back_t(h):
+            b = ps_b.tile([P, S], F32, name="b", tag="b")
+            for t in range(NT):
+                nc.tensor.transpose(out=b[:, t * P:(t + 1) * P], in_=tts[h][:, t * P:(t + 1) * P], identity=ident[:])
+            back[h] = b
+
+        def rope_mul(h):
+            b = back[h]
+            y = yout.tile([P, NT, D], F32, name="y", tag="y")
+            ys[h] = y
+            if h >= NROPE:
+                nc.scalar.copy(out=y[:], in_=b[:].rearrange("p (t d) -> p t d", t=NT))
+                return
+            nc.vector.tensor_tensor(out=y[:], in0=b[:].rearrange("p (t d) -> p t d", t=NT), in1=pe[:, :, 0:D], op=MUL)
+            b4 = b[:].rearrange("p (t i two) -> p t i two", t=NT, two=2)
+            s4 = pe[:, :, D:2 * D].rearrange("p t (i two) -> p t i two", two=2)
+            bp = wrk.tile([P, 2, NT, D // 2], F32, name="bp", tag="bp")
+            nc.vector.tensor_tensor(out=bp[:, 0, :, :], in0=b4[:, :, :, 1], in1=s4[:, :, :, 0], op=MUL)
+            nc.vector.tensor_tensor(out=bp[:, 1, :, :], in0=b4[:, :, :, 0], in1=s4[:, :, :, 1], op=MUL)
+            bps[h] = bp
+
+        def rope_add_store(h):
+            y = ys[h]
+            if h < NROPE:
+                y4 = y[:].rearrange("p t (i two) -> p t i two", two=2)
+                eng = nc.gpsimd if h in GADD else nc.vector
+                eng.tensor_tensor(out=y4, in0=y4, in1=bps[h][:].rearrange("p two t i -> p t i two"), op=ADD)
+            if h < 16:
+                dst = out_0[0, h]
+            elif h < 18:
+                dst = out_1[0, h - 16]
+            else:
+                dst = out_2[0, h - 18]
+            nc.sync.dma_start(out=dst.rearrange("(p t) d -> p t d", t=NT), in_=y[:])
+
+        groups = [list(range(c * HPC, (c + 1) * HPC)) for c in range(NH // HPC)]
+        nc_cycles = len(groups)
+
+        def grp_at(c):
+            return groups[c] if 0 <= c < nc_cycles else []
+
+        pro = [("x", t) for t in range(NT)] + [("w", h) for h in groups[0]]
+        for i, u in enumerate(pro):
+            fwd_t(u)
+            if i == 0:
+                bt = ps_b.tile([P, S], F32, name="bt", tag="b")
+                nc.tensor.transpose(out=bt[:, 0:P], in_=brow32[:], identity=ident[:])
+                nc.vector.tensor_copy(out=bias_col[:, 0:NH], in_=bt[:, 0:NH])
+            f_evac(u, ("s", "v"))
+            if i > 0:
+                quant(pro[i - 1])
+        quant(pro[-1])
+
+        for c in range(nc_cycles + BL):
+            for h in grp_at(c - 1):
+                b_evac(h)
+            for h in grp_at(c + 1):
+                fwd_t(("w", h))
+            for h in grp_at(c - BL):
+                back_t(h)
+            for h in grp_at(c + 1):
+                f_evac(("w", h), ("s", "s"))
+            for h in grp_at(c):
+                mx(h)
+            old = grp_at(c - BL)
+            new = grp_at(c + 1)
+            for i in range(HPC):
+                if i < len(old):
+                    rope_mul(old[i])
+                if i < len(new):
+                    quant(("w", new[i]))
+                if i < len(old):
+                    rope_add_store(old[i])

@@ -24,7 +24,7 @@ FLOPS = 2 * S * NH * D * HID
 
 HPC = 2
 BL = 1
-GADD = []
+GADD = list(range(18))
 
 
 def tile_multiqueryattention_pa_kernel(tc, tensor, w_qkv, b_qkv, pos_emb, out_0, out_1, out_2):
@@ -63,6 +63,7 @@ def tile_multiqueryattention_pa_kernel(tc, tensor, w_qkv, b_qkv, pos_emb, out_0,
         nc.vector.memset(brow32[:], 0.0)
         nc.vector.tensor_copy(out=brow32[0:NH, :], in_=brow[0:NH, :])
         bias_col = const.tile([P, 32], F32, name="bias_col")
+        tb = const.tile([P, 2, S // 2, 2], F32, name="tb")
 
         xc = const.tile([P, NG * S], U32, name="xc", align_bytes=64)
         xs = const.tile([P, NG * S], U8, name="xs", align_bytes=64)
@@ -135,34 +136,41 @@ def tile_multiqueryattention_pa_kernel(tc, tensor, w_qkv, b_qkv, pos_emb, out_0,
                 nc.tensor.transpose(out=b[:, t * P:(t + 1) * P], in_=tts[h][:, t * P:(t + 1) * P], identity=ident[:])
             back[h] = b
 
+        def rope_table():
+            p4 = pe[:].rearrange("p t (s i m) -> p s t i m", s=2, m=2)
+            t5 = tb[:].rearrange("p n (t i) m -> p n t i m", t=NT)
+            nc.vector.tensor_copy(out=t5[:, 0, :, :, 0], in_=p4[:, 0, :, :, 0])
+            nc.vector.tensor_copy(out=t5[:, 0, :, :, 1], in_=p4[:, 1, :, :, 1])
+            nc.vector.tensor_copy(out=t5[:, 1, :, :, 0], in_=p4[:, 1, :, :, 0])
+            nc.vector.tensor_copy(out=t5[:, 1, :, :, 1], in_=p4[:, 0, :, :, 1])
+
         def rope_mul(h):
             b = back[h]
-            y = yout.tile([P, NT, D], F32, name="y", tag="y")
-            ys[h] = y
             if h >= NROPE:
-                nc.scalar.copy(out=y[:], in_=b[:].rearrange("p (t d) -> p t d", t=NT))
+                y = yout.tile([P, S], F32, name="y", tag="y")
+                ys[h] = y
+                nc.scalar.copy(out=y[:], in_=b[:])
                 return
-            nc.vector.tensor_tensor(out=y[:], in0=b[:].rearrange("p (t d) -> p t d", t=NT), in1=pe[:, :, 0:D], op=MUL)
-            b4 = b[:].rearrange("p (t i two) -> p t i two", t=NT, two=2)
-            s4 = pe[:, :, D:2 * D].rearrange("p t (i two) -> p t i two", two=2)
-            bp = wrk.tile([P, 2, NT, D // 2], F32, name="bp", tag="bp")
-            nc.vector.tensor_tensor(out=bp[:, 0, :, :], in0=b4[:, :, :, 1], in1=s4[:, :, :, 0], op=MUL)
-            nc.vector.tensor_tensor(out=bp[:, 1, :, :], in0=b4[:, :, :, 0], in1=s4[:, :, :, 1], op=MUL)
-            bps[h] = bp
+            pr = wrk.tile([P, 2, S // 2, 2], F32, name="pr", tag="pr")
+            b4 = b[:].rearrange("p (c n) -> p n c", n=2).unsqueeze(3).to_broadcast([P, 2, S // 2, 2])
+            nc.vector.tensor_tensor(out=pr[:], in0=b4, in1=tb[:], op=MUL)
+            bps[h] = pr
 
         def rope_add_store(h):
-            y = ys[h]
             if h < NROPE:
-                y4 = y[:].rearrange("p t (i two) -> p t i two", two=2)
+                y = yout.tile([P, S], F32, name="y", tag="y")
+                ys[h] = y
+                pr = bps[h]
                 eng = nc.gpsimd if h in GADD else nc.vector
-                eng.tensor_tensor(out=y4, in0=y4, in1=bps[h][:].rearrange("p two t i -> p t i two"), op=ADD)
+                eng.tensor_tensor(out=y[:].rearrange("p (c m) -> p c m", m=2), in0=pr[:, 0, :, :], in1=pr[:, 1, :, :], op=ADD)
+            y = ys[h]
             if h < 16:
                 dst = out_0[0, h]
             elif h < 18:
                 dst = out_1[0, h - 16]
             else:
                 dst = out_2[0, h - 18]
-            nc.sync.dma_start(out=dst.rearrange("(p t) d -> p t d", t=NT), in_=y[:])
+            nc.sync.dma_start(out=dst.rearrange("(p t) d -> p (t d)", t=NT), in_=y[:])
 
         groups = [list(range(c * HPC, (c + 1) * HPC)) for c in range(NH // HPC)]
         nc_cycles = len(groups)
@@ -193,6 +201,8 @@ def tile_multiqueryattention_pa_kernel(tc, tensor, w_qkv, b_qkv, pos_emb, out_0,
                 f_evac(("w", h), ("s", "s"))
             for h in grp_at(c):
                 mx(h)
+            if c == 0:
+                rope_table()
             old = grp_at(c - BL)
             new = grp_at(c + 1)
             for i in range(HPC):

@@ -21,10 +21,9 @@ NROPE = 18
 NT = S // P
 NG = HID // 512
 FLOPS = 2 * S * NH * D * HID
-
 HPC = 2
-BL = 1
-GADD = list(range(18))
+NCYC = NROPE // HPC
+GADD = list(range(NROPE))
 
 
 def tile_multiqueryattention_pa_kernel(tc, tensor, w_qkv, b_qkv, pos_emb, out_0, out_1, out_2):
@@ -54,8 +53,10 @@ def tile_multiqueryattention_pa_kernel(tc, tensor, w_qkv, b_qkv, pos_emb, out_0,
             wr = raw.tile([P, HID], BF16, name="wraw%d" % h)
             nc.sync.dma_start(out=wr[:], in_=w_qkv[h * D:(h + 1) * D, :])
             units[("w", h)] = wr
-            if h == 1:
+            if h == 3:
                 nc.sync.dma_start(out=pe[:], in_=pos_emb.rearrange("(p t) c -> p t c", t=NT))
+        bias_v = const.tile([P, 2 * D], BF16, name="bias_v")
+        nc.sync.dma_start(out=bias_v[:], in_=b_qkv[NROPE * D:NH * D].partition_broadcast(P))
 
         ident = const.tile([P, P], F32, name="ident")
         make_identity(nc, ident[:])
@@ -67,6 +68,10 @@ def tile_multiqueryattention_pa_kernel(tc, tensor, w_qkv, b_qkv, pos_emb, out_0,
 
         xc = const.tile([P, NG * S], U32, name="xc", align_bytes=64)
         xs = const.tile([P, NG * S], U8, name="xs", align_bytes=64)
+        gv = const.tile([P, 2 * HID], BF16, name="gv", align_bytes=64)
+        vc = const.tile([P, NG * 2 * D], U32, name="vc", align_bytes=64)
+        vs = const.tile([P, NG * 2 * D], U8, name="vs", align_bytes=64)
+        yv = const.tile([P, 2, NT, D], F32, name="yv")
 
         banks = {}
         grouped = {}
@@ -74,8 +79,7 @@ def tile_multiqueryattention_pa_kernel(tc, tensor, w_qkv, b_qkv, pos_emb, out_0,
         acc = {}
         tts = {}
         back = {}
-        ys = {}
-        bps = {}
+        prs = {}
 
         def fwd_t(u):
             src = units[u][:].bitcast(F32)
@@ -89,16 +93,21 @@ def tile_multiqueryattention_pa_kernel(tc, tensor, w_qkv, b_qkv, pos_emb, out_0,
             banks[u] = pair
 
         def f_evac(u, engines):
-            g = grp.tile([P, HID], BF16, name="g", tag="g", align_bytes=64)
-            gw = g[:].bitcast(F32)
+            if u[0] == "w" and u[1] >= NROPE:
+                c0 = (u[1] - NROPE) * D
+                gw = gv[:].bitcast(F32).rearrange("p (g c u) -> p g c u", g=NG, u=2)
+                dsts = [gw[:, 2 * b:2 * b + 2, c0:c0 + D, :] for b in range(2)]
+            else:
+                g = grp.tile([P, HID], BF16, name="g", tag="g", align_bytes=64)
+                grouped[u] = g
+                gw = g[:].bitcast(F32).rearrange("p (g c u) -> p g c u", g=NG, u=2)
+                dsts = [gw[:, 2 * b:2 * b + 2, :, :] for b in range(2)]
             for b in range(2):
-                dst = gw[:, b * 512:(b + 1) * 512].rearrange("p (g r u) -> p g r u", g=2, u=2)
                 src = banks[u][b][:].rearrange("p (g u r) -> p g r u", g=2, u=2)
                 if engines[b] == "s":
-                    nc.scalar.copy(out=dst, in_=src)
+                    nc.scalar.copy(out=dsts[b], in_=src)
                 else:
-                    nc.vector.tensor_copy(out=dst, in_=src)
-            grouped[u] = g
+                    nc.vector.tensor_copy(out=dsts[b], in_=src)
 
         def quant(u):
             g = grouped[u]
@@ -114,6 +123,9 @@ def tile_multiqueryattention_pa_kernel(tc, tensor, w_qkv, b_qkv, pos_emb, out_0,
                 nc.vector.quantize_mx(out=wc[:].bitcast(FP8X4), scales=ws[:], in_=g[:])
                 codes[u[1]] = (wc, ws)
 
+        def quant_v():
+            nc.vector.quantize_mx(out=vc[:].bitcast(FP8X4), scales=vs[:], in_=gv[:])
+
         def mx(h):
             wc, ws = codes[h]
             a = ps_a.tile([P, S], F32, name="a", tag="a")
@@ -124,6 +136,29 @@ def tile_multiqueryattention_pa_kernel(tc, tensor, w_qkv, b_qkv, pos_emb, out_0,
                                     rhs_scale=xs[:, k * S:(k + 1) * S],
                                     start=(k == 0), stop=(k == NG - 1))
             acc[h] = a
+
+        def mx_v(t):
+            if t % 2 == 0:
+                acc[("v", t // 2)] = ps_a.tile([P, S], F32, name="a", tag="a")
+            a = acc[("v", t // 2)]
+            n0 = (t % 2) * 2 * D
+            for k in range(NG):
+                c0 = k * S + t * P
+                nc.tensor.matmul_mx(out=a[:, n0:n0 + 2 * D], lhsT=xc[:, c0:c0 + P].bitcast(FP8X4),
+                                    lhsT_scale=xs[:, c0:c0 + P],
+                                    rhs=vc[:, k * 2 * D:(k + 1) * 2 * D].bitcast(FP8X4),
+                                    rhs_scale=vs[:, k * 2 * D:(k + 1) * 2 * D],
+                                    start=(k == 0), stop=(k == NG - 1))
+
+        def v_add_store(bb):
+            a = acc[("v", bb)]
+            nc.vector.tensor_tensor(
+                out=yv[:].rearrange("p e t d -> p t e d")[:, 2 * bb:2 * bb + 2, :, :],
+                in0=a[:].rearrange("p (t e d) -> p t e d", t=2, e=2),
+                in1=bias_v[:].rearrange("p (e d) -> p e d", e=2).unsqueeze(1).to_broadcast([P, 2, 2, D]),
+                op=ADD)
+            nc.sync.dma_start(out=out_2[0].rearrange("e (p t) d -> p e t d", t=NT)[:, :, 2 * bb:2 * bb + 2, :],
+                              in_=yv[:, :, 2 * bb:2 * bb + 2, :])
 
         def b_evac(h):
             tt = wrk.tile([P, S], F32, name="tt", tag="tt")
@@ -145,40 +180,26 @@ def tile_multiqueryattention_pa_kernel(tc, tensor, w_qkv, b_qkv, pos_emb, out_0,
             nc.vector.tensor_copy(out=t5[:, 1, :, :, 1], in_=p4[:, 0, :, :, 1])
 
         def rope_mul(h):
-            b = back[h]
-            if h >= NROPE:
-                y = yout.tile([P, S], F32, name="y", tag="y")
-                ys[h] = y
-                nc.scalar.copy(out=y[:], in_=b[:])
-                return
             pr = wrk.tile([P, 2, S // 2, 2], F32, name="pr", tag="pr")
-            b4 = b[:].rearrange("p (c n) -> p n c", n=2).unsqueeze(3).to_broadcast([P, 2, S // 2, 2])
+            b4 = back[h][:].rearrange("p (c n) -> p n c", n=2).unsqueeze(3).to_broadcast([P, 2, S // 2, 2])
             nc.vector.tensor_tensor(out=pr[:], in0=b4, in1=tb[:], op=MUL)
-            bps[h] = pr
+            prs[h] = pr
 
-        def rope_add_store(h):
-            if h < NROPE:
-                y = yout.tile([P, S], F32, name="y", tag="y")
-                ys[h] = y
-                pr = bps[h]
-                eng = nc.gpsimd if h in GADD else nc.vector
-                eng.tensor_tensor(out=y[:].rearrange("p (c m) -> p c m", m=2), in0=pr[:, 0, :, :], in1=pr[:, 1, :, :], op=ADD)
-            y = ys[h]
-            if h < 16:
-                dst = out_0[0, h]
-            elif h < 18:
-                dst = out_1[0, h - 16]
-            else:
-                dst = out_2[0, h - 18]
+        def rope_add(h):
+            y = yout.tile([P, S], F32, name="y", tag="y")
+            pr = prs[h]
+            eng = nc.gpsimd if h in GADD else nc.vector
+            eng.tensor_tensor(out=y[:].rearrange("p (c m) -> p c m", m=2), in0=pr[:, 0, :, :], in1=pr[:, 1, :, :], op=ADD)
+            return y
+
+        def store(h, y):
+            dst = out_0[0, h] if h < 16 else out_1[0, h - 16]
             nc.sync.dma_start(out=dst.rearrange("(p t) d -> p (t d)", t=NT), in_=y[:])
 
-        groups = [list(range(c * HPC, (c + 1) * HPC)) for c in range(NH // HPC)]
-        nc_cycles = len(groups)
-
         def grp_at(c):
-            return groups[c] if 0 <= c < nc_cycles else []
+            return list(range(c * HPC, (c + 1) * HPC)) if 0 <= c < NH // HPC else []
 
-        pro = [("x", t) for t in range(NT)] + [("w", h) for h in groups[0]]
+        pro = [("x", t) for t in range(NT)] + [("w", h) for h in grp_at(0)]
         for i, u in enumerate(pro):
             fwd_t(u)
             if i == 0:
@@ -190,12 +211,12 @@ def tile_multiqueryattention_pa_kernel(tc, tensor, w_qkv, b_qkv, pos_emb, out_0,
                 quant(pro[i - 1])
         quant(pro[-1])
 
-        for c in range(nc_cycles + BL):
+        for c in range(NCYC):
             for h in grp_at(c - 1):
                 b_evac(h)
             for h in grp_at(c + 1):
                 fwd_t(("w", h))
-            for h in grp_at(c - BL):
+            for h in grp_at(c - 1):
                 back_t(h)
             for h in grp_at(c + 1):
                 f_evac(("w", h), ("s", "s"))
@@ -203,12 +224,30 @@ def tile_multiqueryattention_pa_kernel(tc, tensor, w_qkv, b_qkv, pos_emb, out_0,
                 mx(h)
             if c == 0:
                 rope_table()
-            old = grp_at(c - BL)
+            old = grp_at(c - 1)
             new = grp_at(c + 1)
             for i in range(HPC):
-                if i < len(old):
+                if old:
                     rope_mul(old[i])
-                if i < len(new):
+                if c + 1 < NCYC:
                     quant(("w", new[i]))
-                if i < len(old):
-                    rope_add_store(old[i])
+                elif i == HPC - 1:
+                    quant_v()
+                if old:
+                    store(old[i], rope_add(old[i]))
+
+        h0, h1 = grp_at(NCYC - 1)
+        b_evac(h0)
+        b_evac(h1)
+        back_t(h0)
+        mx_v(0)
+        back_t(h1)
+        mx_v(1)
+        mx_v(2)
+        mx_v(3)
+        rope_mul(h0)
+        rope_mul(h1)
+        store(h0, rope_add(h0))
+        v_add_store(0)
+        v_add_store(1)
+        store(h1, rope_add(h1))

@@ -23,7 +23,7 @@ NG = HID // 512
 FLOPS = 2 * S * NH * D * HID
 HPC = 2
 NCYC = NROPE // HPC
-GADD = list(range(NROPE))
+GADD = list(range(0, NROPE, 2))
 
 
 def tile_multiqueryattention_pa_kernel(tc, tensor, w_qkv, b_qkv, pos_emb, out_0, out_1, out_2):

@@ -23,7 +23,7 @@ NG = HID // 512
 FLOPS = 2 * S * NH * D * HID
 HPC = 2
 NCYC = NROPE // HPC
-GADD = list(range(0, NROPE, 2))
+GADD = list(range(NROPE - 1))
 
 
 def tile_multiqueryattention_pa_kernel(tc, tensor, w_qkv, b_qkv, pos_emb, out_0, out_1, out_2):
@@ -57,6 +57,15 @@ def tile_multiqueryattention_pa_kernel(tc, tensor, w_qkv, b_qkv, pos_emb, out_0,
                 nc.sync.dma_start(out=pe[:], in_=pos_emb.rearrange("(p t) c -> p t c", t=NT))
         bias_v = const.tile([P, 2 * D], BF16, name="bias_v")
         nc.sync.dma_start(out=bias_v[:], in_=b_qkv[NROPE * D:NH * D].partition_broadcast(P))
+
+        z32 = const.tile([P, S // 2], F32, name="z32")
+        nc.vector.memset(z32[:], 0.0)
+        zb = z32[:].bitcast(BF16)
+        dm = ps_a.tile([P, S], F32, name="dm", tag="a")
+
+        def dummy(n):
+            for i in range(n):
+                nc.tensor.matmul(out=dm[:], lhsT=zb[:, 0:P], rhs=zb, start=True, stop=True)
 
         ident = const.tile([P, P], F32, name="ident")
         make_identity(nc, ident[:])
@@ -200,8 +209,10 @@ def tile_multiqueryattention_pa_kernel(tc, tensor, w_qkv, b_qkv, pos_emb, out_0,
             return list(range(c * HPC, (c + 1) * HPC)) if 0 <= c < NH // HPC else []
 
         pro = [("x", t) for t in range(NT)] + [("w", h) for h in grp_at(0)]
+        dummy(6)
         for i, u in enumerate(pro):
             fwd_t(u)
+            dummy(1)
             if i == 0:
                 bt = ps_b.tile([P, S], F32, name="bt", tag="b")
                 nc.tensor.transpose(out=bt[:, 0:P], in_=brow32[:], identity=ident[:])
@@ -216,6 +227,8 @@ def tile_multiqueryattention_pa_kernel(tc, tensor, w_qkv, b_qkv, pos_emb, out_0,
                 b_evac(h)
             for h in grp_at(c + 1):
                 fwd_t(("w", h))
+                if c == 0:
+                    dummy(1)
             for h in grp_at(c - 1):
                 back_t(h)
             for h in grp_at(c + 1):
@@ -231,7 +244,7 @@ def tile_multiqueryattention_pa_kernel(tc, tensor, w_qkv, b_qkv, pos_emb, out_0,
                     rope_mul(old[i])
                 if c + 1 < NCYC:
                     quant(("w", new[i]))
-                elif i == HPC - 1:
+                elif i == 0:
                     quant_v()
                 if old:
                     store(old[i], rope_add(old[i]))
@@ -248,6 +261,6 @@ def tile_multiqueryattention_pa_kernel(tc, tensor, w_qkv, b_qkv, pos_emb, out_0,
         rope_mul(h0)
         rope_mul(h1)
         store(h0, rope_add(h0))
+        store(h1, rope_add(h1))
         v_add_store(0)
         v_add_store(1)
-        store(h1, rope_add(h1))

@@ -22,6 +22,7 @@ NT = S // P
 NG = HID // 512
 FLOPS = 2 * S * NH * D * HID
 HPC = 2
+PRO_EVAC = (("s", "v"), ("s", "v"), ("s", "s"), ("s", "v"), ("s", "s"), ("s", "s"))
 NCYC = NROPE // HPC
 GADD = list(range(NROPE - 1))
 
@@ -40,14 +41,14 @@ def tile_multiqueryattention_pa_kernel(tc, tensor, w_qkv, b_qkv, pos_emb, out_0,
         ps_b = ctx.enter_context(tc.psum_pool(name="ps_b", bufs=2))
         ctx.enter_context(tc.manual_schedule())
 
-        brow = const.tile([P, D], BF16, name="brow")
-        nc.scalar.dma_start(out=brow[0:NH, :], in_=b_qkv.rearrange("(h d) -> h d", d=D))
         xv = tensor.rearrange("b (p t) k -> (b t) p k", t=NT)
         units = {}
         for t in range(NT):
             xr = raw.tile([P, HID], BF16, name="xraw%d" % t)
             nc.sync.dma_start(out=xr[:], in_=xv[t])
             units[("x", t)] = xr
+        brow = const.tile([P, D], BF16, name="brow")
+        nc.sync.dma_start(out=brow[0:NH, :], in_=b_qkv.rearrange("(h d) -> h d", d=D))
         pe = const.tile([P, NT, 2 * D], BF16, name="pe")
         for h in range(NH):
             wr = raw.tile([P, HID], BF16, name="wraw%d" % h)
@@ -71,7 +72,6 @@ def tile_multiqueryattention_pa_kernel(tc, tensor, w_qkv, b_qkv, pos_emb, out_0,
         make_identity(nc, ident[:])
         brow32 = const.tile([P, P], F32, name="brow32")
         nc.vector.memset(brow32[:], 0.0)
-        nc.vector.tensor_copy(out=brow32[0:NH, :], in_=brow[0:NH, :])
         bias_col = const.tile([P, 32], F32, name="bias_col")
         tb = const.tile([P, 2, S // 2, 2], F32, name="tb")
 
@@ -213,30 +213,29 @@ def tile_multiqueryattention_pa_kernel(tc, tensor, w_qkv, b_qkv, pos_emb, out_0,
         for i, u in enumerate(pro):
             fwd_t(u)
             dummy(1)
-            if i == 0:
-                bt = ps_b.tile([P, S], F32, name="bt", tag="b")
-                nc.tensor.transpose(out=bt[:, 0:P], in_=brow32[:], identity=ident[:])
-                nc.vector.tensor_copy(out=bias_col[:, 0:NH], in_=bt[:, 0:NH])
-            f_evac(u, ("s", "v"))
+            f_evac(u, PRO_EVAC[i])
             if i > 0:
                 quant(pro[i - 1])
         quant(pro[-1])
+        nc.vector.tensor_copy(out=brow32[0:NH, :], in_=brow[0:NH, :])
 
         for c in range(NCYC):
             for h in grp_at(c - 1):
                 b_evac(h)
+            cur = grp_at(c)
+            if c == 0:
+                mx(cur[0])
             for h in grp_at(c + 1):
                 fwd_t(("w", h))
-                if c == 0:
-                    dummy(1)
             for h in grp_at(c - 1):
                 back_t(h)
             for h in grp_at(c + 1):
-                f_evac(("w", h), ("s", "s"))
-            for h in grp_at(c):
+                f_evac(("w", h), ("s", "s") if c else ("s", "v"))
+            for h in cur[1:] if c == 0 else cur:
                 mx(h)
             if c == 0:
-                rope_table()
+                bt = ps_b.tile([P, S], F32, name="bt", tag="b")
+                nc.tensor.transpose(out=bt[:, 0:P], in_=brow32[:], identity=ident[:])
             old = grp_at(c - 1)
             new = grp_at(c + 1)
             for i in range(HPC):
@@ -248,6 +247,9 @@ def tile_multiqueryattention_pa_kernel(tc, tensor, w_qkv, b_qkv, pos_emb, out_0,
                     quant_v()
                 if old:
                     store(old[i], rope_add(old[i]))
+            if c == 0:
+                nc.vector.tensor_copy(out=bias_col[:, 0:NH], in_=bt[:, 0:NH])
+                rope_table()
 
         h0, h1 = grp_at(NCYC - 1)
         b_evac(h0)

@@ -22,7 +22,7 @@ NT = S // P
 NG = HID // 512
 FLOPS = 2 * S * NH * D * HID
 HPC = 2
-PRO_EVAC = (("s", "v"), ("s", "v"), ("s", "s"), ("s", "v"), ("s", "s"), ("s", "s"))
+PRO_EVAC = (("s", "v"), ("s", "v"), ("s", "s"), ("s", "s"), ("s", "s"), ("s", "s"), ("s", "s"), ("s", "s"))
 NCYC = NROPE // HPC
 GADD = list(range(NROPE - 1))
 
@@ -41,28 +41,32 @@ def tile_multiqueryattention_pa_kernel(tc, tensor, w_qkv, b_qkv, pos_emb, out_0,
         ps_b = ctx.enter_context(tc.psum_pool(name="ps_b", bufs=2))
         ctx.enter_context(tc.manual_schedule())
 
-        xv = tensor.rearrange("b (p t) k -> (b t) p k", t=NT)
+        brow = const.tile([P, D], BF16, name="brow")
+        nc.scalar.dma_start(out=brow[0:NH, :], in_=b_qkv.rearrange("(h d) -> h d", d=D))
         units = {}
+
+        def load_w(h):
+            wr = raw.tile([P, HID], BF16, name="wraw%d" % h)
+            nc.sync.dma_start(out=wr[:], in_=w_qkv[h * D:(h + 1) * D, :])
+            units[("w", h)] = wr
+
+        load_w(18)
+        load_w(19)
+        xv = tensor.rearrange("b (p t) k -> (b t) p k", t=NT)
         for t in range(NT):
             xr = raw.tile([P, HID], BF16, name="xraw%d" % t)
             nc.sync.dma_start(out=xr[:], in_=xv[t])
             units[("x", t)] = xr
-        brow = const.tile([P, D], BF16, name="brow")
-        nc.sync.dma_start(out=brow[0:NH, :], in_=b_qkv.rearrange("(h d) -> h d", d=D))
         pe = const.tile([P, NT, 2 * D], BF16, name="pe")
-        for h in range(NH):
-            wr = raw.tile([P, HID], BF16, name="wraw%d" % h)
-            nc.sync.dma_start(out=wr[:], in_=w_qkv[h * D:(h + 1) * D, :])
-            units[("w", h)] = wr
+        for h in range(NROPE):
+            load_w(h)
             if h == 3:
                 nc.sync.dma_start(out=pe[:], in_=pos_emb.rearrange("(p t) c -> p t c", t=NT))
-        bias_v = const.tile([P, 2 * D], BF16, name="bias_v")
-        nc.sync.dma_start(out=bias_v[:], in_=b_qkv[NROPE * D:NH * D].partition_broadcast(P))
 
         z32 = const.tile([P, S // 2], F32, name="z32")
         nc.vector.memset(z32[:], 0.0)
         zb = z32[:].bitcast(BF16)
-        dm = ps_a.tile([P, S], F32, name="dm", tag="a")
+        dm = ps_b.tile([P, S], F32, name="dm", tag="b")
 
         def dummy(n):
             for i in range(n):
@@ -72,6 +76,12 @@ def tile_multiqueryattention_pa_kernel(tc, tensor, w_qkv, b_qkv, pos_emb, out_0,
         make_identity(nc, ident[:])
         brow32 = const.tile([P, P], F32, name="brow32")
         nc.vector.memset(brow32[:], 0.0)
+        brv = const.tile([P, 2 * D], BF16, name="brv")
+        nc.gpsimd.memset(brv[:], 0.0)
+        nc.scalar.dma_start(out=brv[0:1, :], in_=b_qkv[NROPE * D:NH * D].unsqueeze(0))
+        ones = const.tile([P, P], BF16, name="ones")
+        nc.gpsimd.memset(ones[:], 1.0)
+        bias_v = const.tile([P, 2 * D], F32, name="bias_v")
         bias_col = const.tile([P, 32], F32, name="bias_col")
         tb = const.tile([P, 2, S // 2, 2], F32, name="tb")
 
@@ -206,63 +216,66 @@ def tile_multiqueryattention_pa_kernel(tc, tensor, w_qkv, b_qkv, pos_emb, out_0,
             nc.sync.dma_start(out=dst.rearrange("(p t) d -> p (t d)", t=NT), in_=y[:])
 
         def grp_at(c):
-            return list(range(c * HPC, (c + 1) * HPC)) if 0 <= c < NH // HPC else []
+            return list(range(c * HPC, (c + 1) * HPC)) if 0 <= c < NCYC else []
 
-        pro = [("x", t) for t in range(NT)] + [("w", h) for h in grp_at(0)]
-        dummy(6)
+        pro = [("w", 18), ("w", 19)] + [("x", t) for t in range(NT)] + [("w", 0), ("w", 1)]
+        dummy(4)
         for i, u in enumerate(pro):
             fwd_t(u)
-            dummy(1)
+            if i < 3:
+                dummy(1)
+            elif i == 3:
+                bb = ps_b.tile([P, S], F32, name="bb", tag="b")
+                nc.tensor.matmul(out=bb[:, 0:2 * D], lhsT=ones[:], rhs=brv[:], start=True, stop=True)
+                nc.tensor.transpose(out=bb[:, 2 * D:2 * D + P], in_=brow32[:], identity=ident[:])
+            else:
+                mx_v(i - 4)
             f_evac(u, PRO_EVAC[i])
-            if i > 0:
+            if i == 2:
+                quant_v()
+                nc.vector.tensor_copy(out=brow32[0:NH, :], in_=brow[0:NH, :])
+            elif i > 2:
                 quant(pro[i - 1])
+            if i == 3:
+                nc.scalar.copy(out=bias_v[:], in_=bb[:, 0:2 * D])
+                nc.scalar.copy(out=bias_col[:, 0:NH], in_=bb[:, 2 * D:2 * D + NH])
+            elif i == 6:
+                v_add_store(0)
         quant(pro[-1])
-        nc.vector.tensor_copy(out=brow32[0:NH, :], in_=brow[0:NH, :])
+        v_add_store(1)
 
         for c in range(NCYC):
-            for h in grp_at(c - 1):
-                b_evac(h)
+            old = grp_at(c - 1)
             cur = grp_at(c)
+            new = grp_at(c + 1)
+            for h in old:
+                b_evac(h)
             if c == 0:
                 mx(cur[0])
-            for h in grp_at(c + 1):
+            for h in new:
                 fwd_t(("w", h))
-            for h in grp_at(c - 1):
+            for h in old:
                 back_t(h)
-            for h in grp_at(c + 1):
+            for h in new:
                 f_evac(("w", h), ("s", "s") if c else ("s", "v"))
             for h in cur[1:] if c == 0 else cur:
                 mx(h)
-            if c == 0:
-                bt = ps_b.tile([P, S], F32, name="bt", tag="b")
-                nc.tensor.transpose(out=bt[:, 0:P], in_=brow32[:], identity=ident[:])
-            old = grp_at(c - 1)
-            new = grp_at(c + 1)
             for i in range(HPC):
                 if old:
                     rope_mul(old[i])
-                if c + 1 < NCYC:
+                if new:
                     quant(("w", new[i]))
-                elif i == 0:
-                    quant_v()
                 if old:
                     store(old[i], rope_add(old[i]))
             if c == 0:
-                nc.vector.tensor_copy(out=bias_col[:, 0:NH], in_=bt[:, 0:NH])
                 rope_table()
 
         h0, h1 = grp_at(NCYC - 1)
         b_evac(h0)
         b_evac(h1)
         back_t(h0)
-        mx_v(0)
         back_t(h1)
-        mx_v(1)
-        mx_v(2)
-        mx_v(3)
         rope_mul(h0)
         rope_mul(h1)
         store(h0, rope_add(h0))
         store(h1, rope_add(h1))
-        v_add_store(0)
-        v_add_store(1)

@@ -22,7 +22,7 @@ NT = S // P
 NG = HID // 512
 FLOPS = 2 * S * NH * D * HID
 HPC = 2
-PRO_EVAC = (("s", "v"), ("s", "v"), ("s", "s"), ("s", "s"), ("s", "s"), ("s", "s"), ("s", "s"), ("s", "s"))
+PRO_EVAC = (("s", "v"), ("s", "v"), ("s", "s"), ("s", "s"), ("s", "v"), ("s", "s"), ("s", "v"), ("s", "v"))
 NCYC = NROPE // HPC
 GADD = list(range(NROPE - 1))
 
@@ -42,7 +42,11 @@ def tile_multiqueryattention_pa_kernel(tc, tensor, w_qkv, b_qkv, pos_emb, out_0,
         ctx.enter_context(tc.manual_schedule())
 
         brow = const.tile([P, D], BF16, name="brow")
-        nc.scalar.dma_start(out=brow[0:NH, :], in_=b_qkv.rearrange("(h d) -> h d", d=D))
+        nc.scalar.dma_start(out=brow[0:16, :], in_=b_qkv[0:16 * D].rearrange("(h d) -> h d", d=D))
+        nc.scalar.dma_start(out=brow[16:18, :], in_=b_qkv[16 * D:18 * D].rearrange("(h d) -> h d", d=D))
+        brv = const.tile([P, 2 * D], BF16, name="brv")
+        nc.vector.memset(brv[:], 0.0)
+        nc.scalar.dma_start(out=brv[0:1, :], in_=b_qkv[NROPE * D:NH * D].unsqueeze(0))
         units = {}
 
         def load_w(h):
@@ -66,7 +70,7 @@ def tile_multiqueryattention_pa_kernel(tc, tensor, w_qkv, b_qkv, pos_emb, out_0,
         z32 = const.tile([P, S // 2], F32, name="z32")
         nc.vector.memset(z32[:], 0.0)
         zb = z32[:].bitcast(BF16)
-        dm = ps_b.tile([P, S], F32, name="dm", tag="b")
+        dm = ps_a.tile([P, S], F32, name="dm", tag="a")
 
         def dummy(n):
             for i in range(n):
@@ -76,9 +80,6 @@ def tile_multiqueryattention_pa_kernel(tc, tensor, w_qkv, b_qkv, pos_emb, out_0,
         make_identity(nc, ident[:])
         brow32 = const.tile([P, P], F32, name="brow32")
         nc.vector.memset(brow32[:], 0.0)
-        brv = const.tile([P, 2 * D], BF16, name="brv")
-        nc.gpsimd.memset(brv[:], 0.0)
-        nc.scalar.dma_start(out=brv[0:1, :], in_=b_qkv[NROPE * D:NH * D].unsqueeze(0))
         ones = const.tile([P, P], BF16, name="ones")
         nc.gpsimd.memset(ones[:], 1.0)
         bias_v = const.tile([P, 2 * D], F32, name="bias_v")
@@ -156,9 +157,21 @@ def tile_multiqueryattention_pa_kernel(tc, tensor, w_qkv, b_qkv, pos_emb, out_0,
                                     start=(k == 0), stop=(k == NG - 1))
             acc[h] = a
 
+        def mx_half(h, e, pool, tag):
+            wc, ws = codes[h]
+            a = pool.tile([P, S], F32, name=tag, tag=tag)
+            for k in range(NG):
+                c0 = k * S + e * (S // 2)
+                nc.tensor.matmul_mx(out=a[:, 0:S // 2], lhsT=wc[:, k * P:(k + 1) * P].bitcast(FP8X4),
+                                    lhsT_scale=ws[:, k * P:(k + 1) * P],
+                                    rhs=xc[:, c0:c0 + S // 2].bitcast(FP8X4),
+                                    rhs_scale=xs[:, c0:c0 + S // 2],
+                                    start=(k == 0), stop=(k == NG - 1))
+            return a
+
         def mx_v(t):
             if t % 2 == 0:
-                acc[("v", t // 2)] = ps_a.tile([P, S], F32, name="a", tag="a")
+                acc[("v", t // 2)] = ps_b.tile([P, S], F32, name="b", tag="b")
             a = acc[("v", t // 2)]
             n0 = (t % 2) * 2 * D
             for k in range(NG):
@@ -225,41 +238,43 @@ def tile_multiqueryattention_pa_kernel(tc, tensor, w_qkv, b_qkv, pos_emb, out_0,
             if i < 3:
                 dummy(1)
             elif i == 3:
-                bb = ps_b.tile([P, S], F32, name="bb", tag="b")
+                bb = ps_a.tile([P, S], F32, name="bb", tag="a")
                 nc.tensor.matmul(out=bb[:, 0:2 * D], lhsT=ones[:], rhs=brv[:], start=True, stop=True)
                 nc.tensor.transpose(out=bb[:, 2 * D:2 * D + P], in_=brow32[:], identity=ident[:])
             else:
                 mx_v(i - 4)
-            f_evac(u, PRO_EVAC[i])
             if i == 2:
+                nc.vector.tensor_copy(out=brow32[0:NROPE, :], in_=brow[0:NROPE, :])
                 quant_v()
-                nc.vector.tensor_copy(out=brow32[0:NH, :], in_=brow[0:NH, :])
             elif i > 2:
                 quant(pro[i - 1])
-            if i == 3:
-                nc.scalar.copy(out=bias_v[:], in_=bb[:, 0:2 * D])
-                nc.scalar.copy(out=bias_col[:, 0:NH], in_=bb[:, 2 * D:2 * D + NH])
-            elif i == 6:
-                v_add_store(0)
+            f_evac(u, PRO_EVAC[i])
+        nc.scalar.copy(out=bias_col[:, 0:NROPE], in_=bb[:, 2 * D:2 * D + NROPE])
+        nc.scalar.copy(out=bias_v[:], in_=bb[:, 0:2 * D])
         quant(pro[-1])
-        v_add_store(1)
 
-        for c in range(NCYC):
+        for c in range(NCYC - 1):
             old = grp_at(c - 1)
             cur = grp_at(c)
             new = grp_at(c + 1)
-            for h in old:
+            for h in old[1:] if c == 1 else old:
                 b_evac(h)
             if c == 0:
                 mx(cur[0])
+                b_evac(cur[0])
             for h in new:
                 fwd_t(("w", h))
+            if c == 0:
+                mx(cur[1])
             for h in old:
                 back_t(h)
             for h in new:
-                f_evac(("w", h), ("s", "s") if c else ("s", "v"))
-            for h in cur[1:] if c == 0 else cur:
+                f_evac(("w", h), ("s", "s"))
+            for h in cur if c else []:
                 mx(h)
+            if c == 0:
+                v_add_store(0)
+                v_add_store(1)
             for i in range(HPC):
                 if old:
                     rope_mul(old[i])
@@ -270,12 +285,37 @@ def tile_multiqueryattention_pa_kernel(tc, tensor, w_qkv, b_qkv, pos_emb, out_0,
             if c == 0:
                 rope_table()
 
+        p0, p1 = grp_at(NCYC - 2)
         h0, h1 = grp_at(NCYC - 1)
+        b_evac(p0)
+        b_evac(p1)
+        back_t(p0)
+        mx(h0)
+        back_t(p1)
+        a0 = mx_half(h1, 0, ps_a, "a")
         b_evac(h0)
-        b_evac(h1)
+        for h in (p0, p1):
+            rope_mul(h)
+            store(h, rope_add(h))
         back_t(h0)
-        back_t(h1)
         rope_mul(h0)
-        rope_mul(h1)
         store(h0, rope_add(h0))
-        store(h1, rope_add(h1))
+        a1 = mx_half(h1, 1, ps_f, "f")
+        tt = wrk.tile([P, S], F32, name="tt", tag="tt")
+        halves = []
+        for e, acc_e, pool, tag in ((0, a0, ps_b, "b"), (1, a1, ps_f, "f")):
+            c0 = e * 2 * P
+            nc.scalar.activation(out=tt[:, c0:c0 + 2 * P], in_=acc_e[:, 0:2 * P], func=IDENT, bias=bias_col[:, h1:h1 + 1], scale=1.0)
+            b = pool.tile([P, S], F32, name=tag, tag=tag)
+            for q in range(2):
+                nc.tensor.transpose(out=b[:, q * P:(q + 1) * P], in_=tt[:, c0 + q * P:c0 + (q + 1) * P], identity=ident[:])
+            halves.append(b)
+        pr = wrk.tile([P, 2, S // 2, 2], F32, name="pr", tag="pr")
+        y = yout.tile([P, S], F32, name="y", tag="y")
+        for e in range(2):
+            b4 = halves[e][:, 0:2 * P].rearrange("p (c n) -> p n c", n=2).unsqueeze(3).to_broadcast([P, 2, P, 2])
+            nc.vector.tensor_tensor(out=pr[:, :, e * P:(e + 1) * P, :], in0=b4, in1=tb[:, :, e * P:(e + 1) * P, :], op=MUL)
+        for e in range(2):
+            nc.vector.tensor_tensor(out=y[:, e * 2 * P:(e + 1) * 2 * P].rearrange("p (c m) -> p c m", m=2),
+                                    in0=pr[:, 0, e * P:(e + 1) * P, :], in1=pr[:, 1, e * P:(e + 1) * P, :], op=ADD)
+        store(h1, y)

from contextlib import ExitStack

import concourse.mybir as mybir
from concourse.masks import make_identity

F32 = mybir.dt.float32
BF16 = mybir.dt.bfloat16
U32 = mybir.dt.uint32
U8 = mybir.dt.uint8
FP8X4 = mybir.dt.float8_e4m3fn_x4
IDENT = mybir.ActivationFunctionType.Identity
MUL = mybir.AluOpType.mult
ADD = mybir.AluOpType.add

P = 128
S = 512
HID = 2048
D = 128
NH = 20
NROPE = 18
NT = S // P
NG = HID // 512
FLOPS = 2 * S * NH * D * HID
HPC = 2
PRO_EVAC = (("s", "v"), ("s", "v"), ("s", "s"), ("s", "s"), ("s", "v"), ("s", "s"), ("s", "v"), ("s", "v"))
NCYC = NROPE // HPC
GADD = list(range(NROPE - 1))


def tile_multiqueryattention_pa_kernel(tc, tensor, w_qkv, b_qkv, pos_emb, out_0, out_1, out_2):
    nc = tc.nc
    with ExitStack() as ctx:
        const = ctx.enter_context(tc.tile_pool(name="const", bufs=1))
        raw = ctx.enter_context(tc.tile_pool(name="raw", bufs=1))
        grp = ctx.enter_context(tc.tile_pool(name="grp", bufs=4))
        cod = ctx.enter_context(tc.tile_pool(name="cod", bufs=2 * HPC + 1))
        wrk = ctx.enter_context(tc.tile_pool(name="wrk", bufs=2 * HPC))
        yout = ctx.enter_context(tc.tile_pool(name="yout", bufs=8))
        ps_f = ctx.enter_context(tc.psum_pool(name="ps_f", bufs=4))
        ps_a = ctx.enter_context(tc.psum_pool(name="ps_a", bufs=2))
        ps_b = ctx.enter_context(tc.psum_pool(name="ps_b", bufs=2))
        ctx.enter_context(tc.manual_schedule())

        brow = const.tile([P, D], BF16, name="brow")
        nc.scalar.dma_start(out=brow[0:16, :], in_=b_qkv[0:16 * D].rearrange("(h d) -> h d", d=D))
        nc.scalar.dma_start(out=brow[16:18, :], in_=b_qkv[16 * D:18 * D].rearrange("(h d) -> h d", d=D))
        brv = const.tile([P, 2 * D], BF16, name="brv")
        nc.vector.memset(brv[:], 0.0)
        nc.scalar.dma_start(out=brv[0:1, :], in_=b_qkv[NROPE * D:NH * D].unsqueeze(0))
        units = {}

        def load_w(h):
            wr = raw.tile([P, HID], BF16, name="wraw%d" % h)
            nc.sync.dma_start(out=wr[:], in_=w_qkv[h * D:(h + 1) * D, :])
            units[("w", h)] = wr

        load_w(18)
        load_w(19)
        xv = tensor.rearrange("b (p t) k -> (b t) p k", t=NT)
        for t in range(NT):
            xr = raw.tile([P, HID], BF16, name="xraw%d" % t)
            nc.sync.dma_start(out=xr[:], in_=xv[t])
            units[("x", t)] = xr
        pe = const.tile([P, NT, 2 * D], BF16, name="pe")
        for h in range(NROPE):
            load_w(h)
            if h == 3:
                nc.sync.dma_start(out=pe[:], in_=pos_emb.rearrange("(p t) c -> p t c", t=NT))

        z32 = const.tile([P, S // 2], F32, name="z32")
        nc.vector.memset(z32[:], 0.0)
        zb = z32[:].bitcast(BF16)
        dm = ps_a.tile([P, S], F32, name="dm", tag="a")

        def dummy(n):
            for i in range(n):
                nc.tensor.matmul(out=dm[:], lhsT=zb[:, 0:P], rhs=zb, start=True, stop=True)

        ident = const.tile([P, P], F32, name="ident")
        make_identity(nc, ident[:])
        brow32 = const.tile([P, P], F32, name="brow32")
        nc.vector.memset(brow32[:], 0.0)
        ones = const.tile([P, P], BF16, name="ones")
        nc.gpsimd.memset(ones[:], 1.0)
        bias_v = const.tile([P, 2 * D], F32, name="bias_v")
        bias_col = const.tile([P, 32], F32, name="bias_col")
        tb = const.tile([P, 2, S // 2, 2], F32, name="tb")

        xc = const.tile([P, NG * S], U32, name="xc", align_bytes=64)
        xs = const.tile([P, NG * S], U8, name="xs", align_bytes=64)
        gv = const.tile([P, 2 * HID], BF16, name="gv", align_bytes=64)
        vc = const.tile([P, NG * 2 * D], U32, name="vc", align_bytes=64)
        vs = const.tile([P, NG * 2 * D], U8, name="vs", align_bytes=64)
        yv = const.tile([P, 2, NT, D], F32, name="yv")

        banks = {}
        grouped = {}
        codes = {}
        acc = {}
        tts = {}
        back = {}
        prs = {}

        def fwd_t(u):
            src = units[u][:].bitcast(F32)
            pair = []
            for b in range(2):
                f = ps_f.tile([P, 512], F32, name="f", tag="f")
                for q in range(4):
                    j = 4 * b + q
                    nc.tensor.transpose(out=f[:, q * P:(q + 1) * P], in_=src[:, j * P:(j + 1) * P], identity=ident[:])
                pair.append(f)
            banks[u] = pair

        def f_evac(u, engines):
            if u[0] == "w" and u[1] >= NROPE:
                c0 = (u[1] - NROPE) * D
                gw = gv[:].bitcast(F32).rearrange("p (g c u) -> p g c u", g=NG, u=2)
                dsts = [gw[:, 2 * b:2 * b + 2, c0:c0 + D, :] for b in range(2)]
            else:
                g = grp.tile([P, HID], BF16, name="g", tag="g", align_bytes=64)
                grouped[u] = g
                gw = g[:].bitcast(F32).rearrange("p (g c u) -> p g c u", g=NG, u=2)
                dsts = [gw[:, 2 * b:2 * b + 2, :, :] for b in range(2)]
            for b in range(2):
                src = banks[u][b][:].rearrange("p (g u r) -> p g r u", g=2, u=2)
                if engines[b] == "s":
                    nc.scalar.copy(out=dsts[b], in_=src)
                else:
                    nc.vector.tensor_copy(out=dsts[b], in_=src)

        def quant(u):
            g = grouped[u]
            if u[0] == "x":
                t = u[1]
                for k in range(NG):
                    c0 = k * S + t * P
                    nc.vector.quantize_mx(out=xc[:, c0:c0 + P].bitcast(FP8X4), scales=xs[:, c0:c0 + P],
                                          in_=g[:, k * 512:(k + 1) * 512])
            else:
                wc = cod.tile([P, NG * P], U32, name="wc", tag="wc", align_bytes=64)
                ws = cod.tile([P, NG * P], U8, name="ws", tag="ws", align_bytes=64)
                nc.vector.quantize_mx(out=wc[:].bitcast(FP8X4), scales=ws[:], in_=g[:])
                codes[u[1]] = (wc, ws)

        def quant_v():
            nc.vector.quantize_mx(out=vc[:].bitcast(FP8X4), scales=vs[:], in_=gv[:])

        def mx(h):
            wc, ws = codes[h]
            a = ps_a.tile([P, S], F32, name="a", tag="a")
            for k in range(NG):
                nc.tensor.matmul_mx(out=a[:], lhsT=wc[:, k * P:(k + 1) * P].bitcast(FP8X4),
                                    lhsT_scale=ws[:, k * P:(k + 1) * P],
                                    rhs=xc[:, k * S:(k + 1) * S].bitcast(FP8X4),
                                    rhs_scale=xs[:, k * S:(k + 1) * S],
                                    start=(k == 0), stop=(k == NG - 1))
            acc[h] = a

        def mx_half(h, e, pool, tag):
            wc, ws = codes[h]
            a = pool.tile([P, S], F32, name=tag, tag=tag)
            for k in range(NG):
                c0 = k * S + e * (S // 2)
                nc.tensor.matmul_mx(out=a[:, 0:S // 2], lhsT=wc[:, k * P:(k + 1) * P].bitcast(FP8X4),
                                    lhsT_scale=ws[:, k * P:(k + 1) * P],
                                    rhs=xc[:, c0:c0 + S // 2].bitcast(FP8X4),
                                    rhs_scale=xs[:, c0:c0 + S // 2],
                                    start=(k == 0), stop=(k == NG - 1))
            return a

        def mx_v(t):
            if t % 2 == 0:
                acc[("v", t // 2)] = ps_b.tile([P, S], F32, name="b", tag="b")
            a = acc[("v", t // 2)]
            n0 = (t % 2) * 2 * D
            for k in range(NG):
                c0 = k * S + t * P
                nc.tensor.matmul_mx(out=a[:, n0:n0 + 2 * D], lhsT=xc[:, c0:c0 + P].bitcast(FP8X4),
                                    lhsT_scale=xs[:, c0:c0 + P],
                                    rhs=vc[:, k * 2 * D:(k + 1) * 2 * D].bitcast(FP8X4),
                                    rhs_scale=vs[:, k * 2 * D:(k + 1) * 2 * D],
                                    start=(k == 0), stop=(k == NG - 1))

        def v_add_store(bb):
            a = acc[("v", bb)]
            nc.vector.tensor_tensor(
                out=yv[:].rearrange("p e t d -> p t e d")[:, 2 * bb:2 * bb + 2, :, :],
                in0=a[:].rearrange("p (t e d) -> p t e d", t=2, e=2),
                in1=bias_v[:].rearrange("p (e d) -> p e d", e=2).unsqueeze(1).to_broadcast([P, 2, 2, D]),
                op=ADD)
            nc.sync.dma_start(out=out_2[0].rearrange("e (p t) d -> p e t d", t=NT)[:, :, 2 * bb:2 * bb + 2, :],
                              in_=yv[:, :, 2 * bb:2 * bb + 2, :])

        def b_evac(h):
            tt = wrk.tile([P, S], F32, name="tt", tag="tt")
            nc.scalar.activation(out=tt[:], in_=acc[h][:], func=IDENT, bias=bias_col[:, h:h + 1], scale=1.0)
            tts[h] = tt

        def back_t(h):
            b = ps_b.tile([P, S], F32, name="b", tag="b")
            for t in range(NT):
                nc.tensor.transpose(out=b[:, t * P:(t + 1) * P], in_=tts[h][:, t * P:(t + 1) * P], identity=ident[:])
            back[h] = b

        def rope_table():
            p4 = pe[:].rearrange("p t (s i m) -> p s t i m", s=2, m=2)
            t5 = tb[:].rearrange("p n (t i) m -> p n t i m", t=NT)
            nc.vector.tensor_copy(out=t5[:, 0, :, :, 0], in_=p4[:, 0, :, :, 0])
            nc.vector.tensor_copy(out=t5[:, 0, :, :, 1], in_=p4[:, 1, :, :, 1])
            nc.vector.tensor_copy(out=t5[:, 1, :, :, 0], in_=p4[:, 1, :, :, 0])
            nc.vector.tensor_copy(out=t5[:, 1, :, :, 1], in_=p4[:, 0, :, :, 1])

        def rope_mul(h):
            pr = wrk.tile([P, 2, S // 2, 2], F32, name="pr", tag="pr")
            b4 = back[h][:].rearrange("p (c n) -> p n c", n=2).unsqueeze(3).to_broadcast([P, 2, S // 2, 2])
            nc.vector.tensor_tensor(out=pr[:], in0=b4, in1=tb[:], op=MUL)
            prs[h] = pr

        def rope_add(h):
            y = yout.tile([P, S], F32, name="y", tag="y")
            pr = prs[h]
            eng = nc.gpsimd if h in GADD else nc.vector
            eng.tensor_tensor(out=y[:].rearrange("p (c m) -> p c m", m=2), in0=pr[:, 0, :, :], in1=pr[:, 1, :, :], op=ADD)
            return y

        def store(h, y):
            dst = out_0[0, h] if h < 16 else out_1[0, h - 16]
            nc.sync.dma_start(out=dst.rearrange("(p t) d -> p (t d)", t=NT), in_=y[:])

        def grp_at(c):
            return list(range(c * HPC, (c + 1) * HPC)) if 0 <= c < NCYC else []

        pro = [("w", 18), ("w", 19)] + [("x", t) for t in range(NT)] + [("w", 0), ("w", 1)]
        dummy(4)
        for i, u in enumerate(pro):
            fwd_t(u)
            if i < 3:
                dummy(1)
            elif i == 3:
                bb = ps_a.tile([P, S], F32, name="bb", tag="a")
                nc.tensor.matmul(out=bb[:, 0:2 * D], lhsT=ones[:], rhs=brv[:], start=True, stop=True)
                nc.tensor.transpose(out=bb[:, 2 * D:2 * D + P], in_=brow32[:], identity=ident[:])
            else:
                mx_v(i - 4)
            if i == 2:
                nc.vector.tensor_copy(out=brow32[0:NROPE, :], in_=brow[0:NROPE, :])
                quant_v()
            elif i > 2:
                quant(pro[i - 1])
            f_evac(u, PRO_EVAC[i])
        nc.scalar.copy(out=bias_col[:, 0:NROPE], in_=bb[:, 2 * D:2 * D + NROPE])
        nc.scalar.copy(out=bias_v[:], in_=bb[:, 0:2 * D])
        quant(pro[-1])

        for c in range(NCYC - 1):
            old = grp_at(c - 1)
            cur = grp_at(c)
            new = grp_at(c + 1)
            for h in old[1:] if c == 1 else old:
                b_evac(h)
            if c == 0:
                mx(cur[0])
                b_evac(cur[0])
            for h in new:
                fwd_t(("w", h))
            if c == 0:
                mx(cur[1])
            for h in old:
                back_t(h)
            for h in new:
                f_evac(("w", h), ("s", "s"))
            for h in cur if c else []:
                mx(h)
            if c == 0:
                v_add_store(0)
                v_add_store(1)
            for i in range(HPC):
                if old:
                    rope_mul(old[i])
                if new:
                    quant(("w", new[i]))
                if old:
                    store(old[i], rope_add(old[i]))
            if c == 0:
                rope_table()

        p0, p1 = grp_at(NCYC - 2)
        h0, h1 = grp_at(NCYC - 1)
        b_evac(p0)
        b_evac(p1)
        back_t(p0)
        mx(h0)
        back_t(p1)
        a0 = mx_half(h1, 0, ps_a, "a")
        b_evac(h0)
        for h in (p0, p1):
            rope_mul(h)
            store(h, rope_add(h))
        back_t(h0)
        rope_mul(h0)
        store(h0, rope_add(h0))
        a1 = mx_half(h1, 1, ps_f, "f")
        tt = wrk.tile([P, S], F32, name="tt", tag="tt")
        halves = []
        for e, acc_e, pool, tag in ((0, a0, ps_b, "b"), (1, a1, ps_f, "f")):
            c0 = e * 2 * P
            nc.scalar.activation(out=tt[:, c0:c0 + 2 * P], in_=acc_e[:, 0:2 * P], func=IDENT, bias=bias_col[:, h1:h1 + 1], scale=1.0)
            b = pool.tile([P, S], F32, name=tag, tag=tag)
            for q in range(2):
                nc.tensor.transpose(out=b[:, q * P:(q + 1) * P], in_=tt[:, c0 + q * P:c0 + (q + 1) * P], identity=ident[:])
            halves.append(b)
        pr = wrk.tile([P, 2, S // 2, 2], F32, name="pr", tag="pr")
        y = yout.tile([P, S], F32, name="y", tag="y")
        for e in range(2):
            b4 = halves[e][:, 0:2 * P].rearrange("p (c n) -> p n c", n=2).unsqueeze(3).to_broadcast([P, 2, P, 2])
            nc.vector.tensor_tensor(out=pr[:, :, e * P:(e + 1) * P, :], in0=b4, in1=tb[:, :, e * P:(e + 1) * P, :], op=MUL)
        for e in range(2):
            nc.vector.tensor_tensor(out=y[:, e * 2 * P:(e + 1) * 2 * P].rearrange("p (c m) -> p c m", m=2),
                                    in0=pr[:, 0, e * P:(e + 1) * P, :], in1=pr[:, 1, e * P:(e + 1) * P, :], op=ADD)
        store(h1, y)
